import numpy as np
import ml_dtypes

BF16 = ml_dtypes.bfloat16


def bf(x):
    return np.asarray(x, np.float32).astype(BF16)


def f32(x):
    return np.asarray(x, np.float32)


def f64(x):
    return np.asarray(x).astype(np.float64)


def striped(idx):
    return np.tile(idx.reshape(-1, 16).T, (8, 1))


C, S, N, M1, M2 = 256, 512, 256, 256, 128
LEAKY = 0.2


def leaky(v):
    return np.maximum(v, LEAKY * v)


def setup_inputs():
    return {"maps": f32(np.random.standard_normal((C, S))), "fc1_w": bf(np.random.standard_normal((C, M1)) / np.sqrt(C)), "fc1_b": f32(0.1 * np.random.standard_normal((M1, 1))), "fc2_w": bf(np.random.standard_normal((M1, M2)) / np.sqrt(M1)), "fc2_b": f32(0.1 * np.random.standard_normal((M2, 1))), "offs": striped(np.random.permutation(S)[:N])}


def reference(maps, fc1_w, fc1_b, fc2_w, fc2_b, offs):
    idx = offs[:16].T.reshape(-1)
    z = f64(maps)[:, idx]
    h = leaky(f64(fc1_w).T @ z + f64(fc1_b))
    return leaky(f64(fc2_w).T @ h + f64(fc2_b))

@@ -1,0 +1,68 @@
+import concourse.mybir as mybir
+
+P = 128
+C, S, N, M1, M2 = 256, 512, 256, 256, 128
+C_BLOCKS = C // P
+M_BLOCKS = M1 // P
+SLOPE = 0.2
+
+FLOPS = 2 * C * M1 * N + 2 * M1 * M2 * N
+
+F32, BF16, U16 = mybir.dt.float32, mybir.dt.bfloat16, mybir.dt.uint16
+COPY = mybir.ActivationFunctionType.Copy
+IDENTITY = mybir.ActivationFunctionType.Identity
+MULT, MAX = mybir.AluOpType.mult, mybir.AluOpType.max
+
+
+def bias_then_leaky(nc, pool, result, product, bias, name):
+    biased = pool.tile([P, N], F32, name=name)
+    nc.scalar.activation(biased[:], product[:], IDENTITY, bias=bias[:])
+    nc.vector.scalar_tensor_tensor(result[:], biased[:], SLOPE, biased[:], MULT, MAX)
+
+
+def tile_rlf_kernel(tc, maps, fc1_w, fc1_b, fc2_w, fc2_b, offs, out):
+    nc = tc.nc
+    with tc.tile_pool(name="held", bufs=1) as held, tc.psum_pool(name="psum", bufs=1) as psum:
+        offsets = held.tile([P, N // 16], U16, name="offsets")
+        nc.sync.dma_start(offsets[:], offs)
+        stored = [held.tile([P, S], F32, name=f"stored{k}") for k in range(C_BLOCKS)]
+        for k in range(C_BLOCKS):
+            nc.sync.dma_start(stored[k][:], maps[k * P : (k + 1) * P, :])
+        w1 = held.tile([P, C_BLOCKS, M1], BF16, name="w1")
+        nc.scalar.dma_start(w1[:], fc1_w.rearrange("(k p) m -> p k m", p=P))
+        w2 = held.tile([P, M_BLOCKS, M2], BF16, name="w2")
+        nc.scalar.dma_start(w2[:], fc2_w.rearrange("(k p) q -> p k q", p=P))
+        b1 = [held.tile([P, 1], F32, name=f"b1_{m}") for m in range(M_BLOCKS)]
+        for m in range(M_BLOCKS):
+            nc.gpsimd.dma_start(b1[m][:], fc1_b[m * P : (m + 1) * P, :])
+        b2 = held.tile([P, 1], F32, name="b2")
+        nc.gpsimd.dma_start(b2[:], fc2_b)
+
+        z_bf16 = []
+        for k in range(C_BLOCKS):
+            z = held.tile([P, N], F32, name=f"z{k}")
+            nc.scalar.activation(z[:], stored[k][:].indirect(offsets[:]), COPY)
+            rounded = held.tile([P, N], BF16, name=f"z_bf16_{k}")
+            nc.vector.tensor_copy(rounded[:], z[:])
+            z_bf16.append(rounded)
+
+        product1 = [psum.tile([P, N], F32, name=f"product1_{m}") for m in range(M_BLOCKS)]
+        for k in range(C_BLOCKS):
+            for m in range(M_BLOCKS):
+                nc.tensor.matmul(
+                    product1[m][:],
+                    w1[:, k, m * P : (m + 1) * P],
+                    z_bf16[k][:],
+                    start=(k == 0),
+                    stop=(k == C_BLOCKS - 1),
+                )
+        h = [held.tile([P, N], BF16, name=f"h{m}") for m in range(M_BLOCKS)]
+        for m in range(M_BLOCKS):
+            bias_then_leaky(nc, held, h[m], product1[m], b1[m], f"biased1_{m}")
+
+        product2 = psum.tile([P, N], F32, name="product2")
+        for m in range(M_BLOCKS):
+            nc.tensor.matmul(product2[:], w2[:, m, :], h[m][:], start=(m == 0), stop=(m == M_BLOCKS - 1))
+        result = held.tile([P, N], F32, name="result")
+        bias_then_leaky(nc, held, result, product2, b2, "biased2")
+        nc.sync.dma_start(out, result[:])

@@ -38,6 +38,11 @@ def tile_rlf_kernel(tc, maps, fc1_w, fc1_b, fc2_w, fc2_b, offs, out):
         b2 = held.tile([P, 1], F32, name="b2")
         nc.gpsimd.dma_start(b2[:], fc2_b)
 
+        warm = held.tile([P, 1], F32, name="warm")
+        nc.vector.memset(warm[:], 0.0)
+        warmed = held.tile([P, 1], F32, name="warmed")
+        nc.scalar.activation(warmed[:], warm[:], COPY)
+
         z_bf16 = []
         for k in range(C_BLOCKS):
             z = held.tile([P, N], F32, name=f"z{k}")

@@ -10,14 +10,13 @@ FLOPS = 2 * C * M1 * N + 2 * M1 * M2 * N
 
 F32, BF16, U16 = mybir.dt.float32, mybir.dt.bfloat16, mybir.dt.uint16
 COPY = mybir.ActivationFunctionType.Copy
-IDENTITY = mybir.ActivationFunctionType.Identity
-MULT, MAX = mybir.AluOpType.mult, mybir.AluOpType.max
+MAX = mybir.AluOpType.max
 
 
-def bias_then_leaky(nc, pool, result, product, bias, name):
-    biased = pool.tile([P, N], F32, name=name)
-    nc.scalar.activation(biased[:], product[:], IDENTITY, bias=bias[:])
-    nc.vector.scalar_tensor_tensor(result[:], biased[:], SLOPE, biased[:], MULT, MAX)
+def leaky(nc, pool, result, biased, name):
+    scaled = pool.tile([P, N], F32, name=name)
+    nc.scalar.activation(scaled[:], biased[:], COPY, scale=SLOPE)
+    nc.vector.tensor_tensor(result[:], biased[:], scaled[:], MAX)
 
 
 def tile_rlf_kernel(tc, maps, fc1_w, fc1_b, fc2_w, fc2_b, offs, out):
@@ -29,19 +28,24 @@ def tile_rlf_kernel(tc, maps, fc1_w, fc1_b, fc2_w, fc2_b, offs, out):
         for k in range(C_BLOCKS):
             nc.sync.dma_start(stored[k][:], maps[k * P : (k + 1) * P, :])
         w1 = held.tile([P, C_BLOCKS, M1], BF16, name="w1")
-        nc.scalar.dma_start(w1[:], fc1_w.rearrange("(k p) m -> p k m", p=P))
+        nc.sync.dma_start(w1[:], fc1_w.rearrange("(k p) m -> p k m", p=P))
         w2 = held.tile([P, M_BLOCKS, M2], BF16, name="w2")
-        nc.scalar.dma_start(w2[:], fc2_w.rearrange("(k p) q -> p k q", p=P))
-        b1 = [held.tile([P, 1], F32, name=f"b1_{m}") for m in range(M_BLOCKS)]
-        for m in range(M_BLOCKS):
-            nc.gpsimd.dma_start(b1[m][:], fc1_b[m * P : (m + 1) * P, :])
-        b2 = held.tile([P, 1], F32, name="b2")
-        nc.gpsimd.dma_start(b2[:], fc2_b)
+        nc.sync.dma_start(w2[:], fc2_w.rearrange("(k p) q -> p k q", p=P))
+        b1_row = held.tile([1, M1], F32, name="b1_row")
+        nc.scalar.dma_start(b1_row[:], fc1_b.rearrange("m o -> o m"))
+        b2_row = held.tile([1, M2], F32, name="b2_row")
+        nc.scalar.dma_start(b2_row[:], fc2_b.rearrange("q o -> o q"))
+        ones_row = held.tile([1, N], F32, name="ones_row")
+        nc.vector.memset(ones_row[:], 1.0)
 
-        warm = held.tile([P, 1], F32, name="warm")
-        nc.vector.memset(warm[:], 0.0)
-        warmed = held.tile([P, 1], F32, name="warmed")
-        nc.scalar.activation(warmed[:], warm[:], COPY)
+        warmed = held.tile([1, 1], F32, name="warmed")
+        nc.scalar.activation(warmed[:], ones_row[:, 0:1], COPY)
+
+        biased1 = [psum.tile([P, N], F32, name=f"biased1_{m}") for m in range(M_BLOCKS)]
+        for m in range(M_BLOCKS):
+            nc.tensor.matmul(biased1[m][:], b1_row[:, m * P : (m + 1) * P], ones_row[:], start=True, stop=False)
+        biased2 = psum.tile([P, N], F32, name="biased2")
+        nc.tensor.matmul(biased2[:], b2_row[:], ones_row[:], start=True, stop=False)
 
         z_bf16 = []
         for k in range(C_BLOCKS):
@@ -51,23 +55,21 @@ def tile_rlf_kernel(tc, maps, fc1_w, fc1_b, fc2_w, fc2_b, offs, out):
             nc.vector.tensor_copy(rounded[:], z[:])
             z_bf16.append(rounded)
 
-        product1 = [psum.tile([P, N], F32, name=f"product1_{m}") for m in range(M_BLOCKS)]
         for k in range(C_BLOCKS):
             for m in range(M_BLOCKS):
                 nc.tensor.matmul(
-                    product1[m][:],
+                    biased1[m][:],
                     w1[:, k, m * P : (m + 1) * P],
                     z_bf16[k][:],
-                    start=(k == 0),
+                    start=False,
                     stop=(k == C_BLOCKS - 1),
                 )
         h = [held.tile([P, N], BF16, name=f"h{m}") for m in range(M_BLOCKS)]
         for m in range(M_BLOCKS):
-            bias_then_leaky(nc, held, h[m], product1[m], b1[m], f"biased1_{m}")
+            leaky(nc, held, h[m], biased1[m], f"scaled1_{m}")
 
-        product2 = psum.tile([P, N], F32, name="product2")
         for m in range(M_BLOCKS):
-            nc.tensor.matmul(product2[:], w2[:, m, :], h[m][:], start=(m == 0), stop=(m == M_BLOCKS - 1))
+            nc.tensor.matmul(biased2[:], w2[:, m, :], h[m][:], start=False, stop=(m == M_BLOCKS - 1))
         result = held.tile([P, N], F32, name="result")
-        bias_then_leaky(nc, held, result, product2, b2, "biased2")
+        leaky(nc, held, result, biased2, "scaled2")
         nc.sync.dma_start(out, result[:])

@@ -4,19 +4,22 @@ P = 128
 C, S, N, M1, M2 = 256, 512, 256, 256, 128
 C_BLOCKS = C // P
 M_BLOCKS = M1 // P
+PIECES = 2
+W = N // PIECES
 SLOPE = 0.2
 
 FLOPS = 2 * C * M1 * N + 2 * M1 * M2 * N
 
 F32, BF16, U16 = mybir.dt.float32, mybir.dt.bfloat16, mybir.dt.uint16
 COPY = mybir.ActivationFunctionType.Copy
-MAX = mybir.AluOpType.max
+IDENTITY = mybir.ActivationFunctionType.Identity
+MULT, MAX = mybir.AluOpType.mult, mybir.AluOpType.max
 
 
-def leaky(nc, pool, result, biased, name):
-    scaled = pool.tile([P, N], F32, name=name)
-    nc.scalar.activation(scaled[:], biased[:], COPY, scale=SLOPE)
-    nc.vector.tensor_tensor(result[:], biased[:], scaled[:], MAX)
+def bias_then_leaky(nc, pool, result, product, bias, name):
+    biased = pool.tile([P, W], F32, name=name)
+    nc.scalar.activation(biased[:], product[:], IDENTITY, bias=bias[:])
+    nc.vector.scalar_tensor_tensor(result[:], biased[:], SLOPE, biased[:], MULT, MAX)
 
 
 def tile_rlf_kernel(tc, maps, fc1_w, fc1_b, fc2_w, fc2_b, offs, out):
@@ -28,48 +31,49 @@ def tile_rlf_kernel(tc, maps, fc1_w, fc1_b, fc2_w, fc2_b, offs, out):
         for k in range(C_BLOCKS):
             nc.sync.dma_start(stored[k][:], maps[k * P : (k + 1) * P, :])
         w1 = held.tile([P, C_BLOCKS, M1], BF16, name="w1")
-        nc.sync.dma_start(w1[:], fc1_w.rearrange("(k p) m -> p k m", p=P))
+        nc.scalar.dma_start(w1[:], fc1_w.rearrange("(k p) m -> p k m", p=P))
         w2 = held.tile([P, M_BLOCKS, M2], BF16, name="w2")
-        nc.sync.dma_start(w2[:], fc2_w.rearrange("(k p) q -> p k q", p=P))
-        b1_row = held.tile([1, M1], F32, name="b1_row")
-        nc.scalar.dma_start(b1_row[:], fc1_b.rearrange("m o -> o m"))
-        b2_row = held.tile([1, M2], F32, name="b2_row")
-        nc.scalar.dma_start(b2_row[:], fc2_b.rearrange("q o -> o q"))
-        ones_row = held.tile([1, N], F32, name="ones_row")
-        nc.vector.memset(ones_row[:], 1.0)
-
-        warmed = held.tile([1, 1], F32, name="warmed")
-        nc.scalar.activation(warmed[:], ones_row[:, 0:1], COPY)
-
-        biased1 = [psum.tile([P, N], F32, name=f"biased1_{m}") for m in range(M_BLOCKS)]
+        nc.scalar.dma_start(w2[:], fc2_w.rearrange("(k p) q -> p k q", p=P))
+        b1 = [held.tile([P, 1], F32, name=f"b1_{m}") for m in range(M_BLOCKS)]
         for m in range(M_BLOCKS):
-            nc.tensor.matmul(biased1[m][:], b1_row[:, m * P : (m + 1) * P], ones_row[:], start=True, stop=False)
-        biased2 = psum.tile([P, N], F32, name="biased2")
-        nc.tensor.matmul(biased2[:], b2_row[:], ones_row[:], start=True, stop=False)
+            nc.gpsimd.dma_start(b1[m][:], fc1_b[m * P : (m + 1) * P, :])
+        b2 = held.tile([P, 1], F32, name="b2")
+        nc.gpsimd.dma_start(b2[:], fc2_b)
 
-        z_bf16 = []
-        for k in range(C_BLOCKS):
-            z = held.tile([P, N], F32, name=f"z{k}")
-            nc.scalar.activation(z[:], stored[k][:].indirect(offsets[:]), COPY)
-            rounded = held.tile([P, N], BF16, name=f"z_bf16_{k}")
-            nc.vector.tensor_copy(rounded[:], z[:])
-            z_bf16.append(rounded)
+        warm = held.tile([P, 1], F32, name="warm")
+        nc.vector.memset(warm[:], 0.0)
+        warmed = held.tile([P, 1], F32, name="warmed")
+        nc.scalar.activation(warmed[:], warm[:], COPY)
 
+        product1 = [
+            [psum.tile([P, W], F32, name=f"product1_{i}_{m}") for m in range(M_BLOCKS)] for i in range(PIECES)
+        ]
         for k in range(C_BLOCKS):
+            for i in range(PIECES):
+                z = held.tile([P, W], F32, name=f"z_{k}_{i}")
+                piece_of_list = offsets[:, i * (W // 16) : (i + 1) * (W // 16)]
+                nc.scalar.activation(z[:], stored[k][:].indirect(piece_of_list), COPY)
+                z_bf16 = held.tile([P, W], BF16, name=f"z_bf16_{k}_{i}")
+                nc.vector.tensor_copy(z_bf16[:], z[:])
+                for m in range(M_BLOCKS):
+                    nc.tensor.matmul(
+                        product1[i][m][:],
+                        w1[:, k, m * P : (m + 1) * P],
+                        z_bf16[:],
+                        start=(k == 0),
+                        stop=(k == C_BLOCKS - 1),
+                    )
+
+        h = [[held.tile([P, W], BF16, name=f"h_{i}_{m}") for m in range(M_BLOCKS)] for i in range(PIECES)]
+        for i in range(PIECES):
             for m in range(M_BLOCKS):
-                nc.tensor.matmul(
-                    biased1[m][:],
-                    w1[:, k, m * P : (m + 1) * P],
-                    z_bf16[k][:],
-                    start=False,
-                    stop=(k == C_BLOCKS - 1),
-                )
-        h = [held.tile([P, N], BF16, name=f"h{m}") for m in range(M_BLOCKS)]
-        for m in range(M_BLOCKS):
-            leaky(nc, held, h[m], biased1[m], f"scaled1_{m}")
+                bias_then_leaky(nc, held, h[i][m], product1[i][m], b1[m], f"biased1_{i}_{m}")
 
-        for m in range(M_BLOCKS):
-            nc.tensor.matmul(biased2[:], w2[:, m, :], h[m][:], start=False, stop=(m == M_BLOCKS - 1))
-        result = held.tile([P, N], F32, name="result")
-        leaky(nc, held, result, biased2, "scaled2")
-        nc.sync.dma_start(out, result[:])
+        product2 = [psum.tile([P, W], F32, name=f"product2_{i}") for i in range(PIECES)]
+        for i in range(PIECES):
+            for m in range(M_BLOCKS):
+                nc.tensor.matmul(product2[i][:], w2[:, m, :], h[i][m][:], start=(m == 0), stop=(m == M_BLOCKS - 1))
+        for i in range(PIECES):
+            result = held.tile([P, W], F32, name=f"result_{i}")
+            bias_then_leaky(nc, held, result, product2[i], b2, f"biased2_{i}")
+            nc.sync.dma_start(out[:, i * W : (i + 1) * W], result[:])

@@ -18,7 +18,7 @@ MULT, MAX = mybir.AluOpType.mult, mybir.AluOpType.max
 
 def bias_then_leaky(nc, pool, result, product, bias, name):
     biased = pool.tile([P, W], F32, name=name)
-    nc.scalar.activation(biased[:], product[:], IDENTITY, bias=bias[:])
+    nc.scalar.activation(biased[:], product[:], IDENTITY, bias=bias)
     nc.vector.scalar_tensor_tensor(result[:], biased[:], SLOPE, biased[:], MULT, MAX)
 
 
@@ -28,17 +28,17 @@ def tile_rlf_kernel(tc, maps, fc1_w, fc1_b, fc2_w, fc2_b, offs, out):
         offsets = held.tile([P, N // 16], U16, name="offsets")
         nc.sync.dma_start(offsets[:], offs)
         stored = [held.tile([P, S], F32, name=f"stored{k}") for k in range(C_BLOCKS)]
-        for k in range(C_BLOCKS):
-            nc.sync.dma_start(stored[k][:], maps[k * P : (k + 1) * P, :])
+        nc.scalar.dma_start(stored[0][:], maps[0:P, :])
+        nc.sync.dma_start(stored[1][:], maps[P : 2 * P, :])
         w1 = held.tile([P, C_BLOCKS, M1], BF16, name="w1")
-        nc.scalar.dma_start(w1[:], fc1_w.rearrange("(k p) m -> p k m", p=P))
+        nc.sync.dma_start(w1[:], fc1_w.rearrange("(k p) m -> p k m", p=P))
         w2 = held.tile([P, M_BLOCKS, M2], BF16, name="w2")
-        nc.scalar.dma_start(w2[:], fc2_w.rearrange("(k p) q -> p k q", p=P))
-        b1 = [held.tile([P, 1], F32, name=f"b1_{m}") for m in range(M_BLOCKS)]
-        for m in range(M_BLOCKS):
-            nc.gpsimd.dma_start(b1[m][:], fc1_b[m * P : (m + 1) * P, :])
+        nc.sync.dma_start(w2[:], fc2_w.rearrange("(k p) q -> p k q", p=P))
+        b1 = held.tile([P, M_BLOCKS], F32, name="b1")
+        with nc.allow_non_contiguous_dma(reason="a bias has one element to a partition"):
+            nc.gpsimd.dma_start(b1[:], fc1_b.rearrange("(m p) o -> p (m o)", p=P))
         b2 = held.tile([P, 1], F32, name="b2")
-        nc.gpsimd.dma_start(b2[:], fc2_b)
+        nc.scalar.dma_start(b2[:], fc2_b)
 
         warm = held.tile([P, 1], F32, name="warm")
         nc.vector.memset(warm[:], 0.0)
@@ -67,7 +67,7 @@ def tile_rlf_kernel(tc, maps, fc1_w, fc1_b, fc2_w, fc2_b, offs, out):
         h = [[held.tile([P, W], BF16, name=f"h_{i}_{m}") for m in range(M_BLOCKS)] for i in range(PIECES)]
         for i in range(PIECES):
             for m in range(M_BLOCKS):
-                bias_then_leaky(nc, held, h[i][m], product1[i][m], b1[m], f"biased1_{i}_{m}")
+                bias_then_leaky(nc, held, h[i][m], product1[i][m], b1[:, m : m + 1], f"biased1_{i}_{m}")
 
         product2 = [psum.tile([P, W], F32, name=f"product2_{i}") for i in range(PIECES)]
         for i in range(PIECES):
@@ -75,5 +75,5 @@ def tile_rlf_kernel(tc, maps, fc1_w, fc1_b, fc2_w, fc2_b, offs, out):
                 nc.tensor.matmul(product2[i][:], w2[:, m, :], h[i][m][:], start=(m == 0), stop=(m == M_BLOCKS - 1))
         for i in range(PIECES):
             result = held.tile([P, W], F32, name=f"result_{i}")
-            bias_then_leaky(nc, held, result, product2[i], b2, f"biased2_{i}")
+            bias_then_leaky(nc, held, result, product2[i], b2[:], f"biased2_{i}")
             nc.sync.dma_start(out[:, i * W : (i + 1) * W], result[:])

@@ -6,6 +6,8 @@ C_BLOCKS = C // P
 M_BLOCKS = M1 // P
 PIECES = 2
 W = N // PIECES
+WARM_COLUMNS = 512
+WARM_MATMULS = 6
 SLOPE = 0.2
 
 FLOPS = 2 * C * M1 * N + 2 * M1 * M2 * N
@@ -44,6 +46,12 @@ def tile_rlf_kernel(tc, maps, fc1_w, fc1_b, fc2_w, fc2_b, offs, out):
         nc.vector.memset(warm[:], 0.0)
         warmed = held.tile([P, 1], F32, name="warmed")
         nc.scalar.activation(warmed[:], warm[:], COPY)
+
+        zeros = held.tile([P, WARM_COLUMNS], BF16, name="zeros")
+        nc.vector.memset(zeros[:], 0.0)
+        unread = psum.tile([P, WARM_COLUMNS], F32, name="unread")
+        for repeat in range(WARM_MATMULS):
+            nc.tensor.matmul(unread[:], zeros[:, 0:P], zeros[:], start=True, stop=True)
 
         product1 = [
             [psum.tile([P, W], F32, name=f"product1_{i}_{m}") for m in range(M_BLOCKS)] for i in range(PIECES)

@@ -31,6 +31,8 @@ def tile_rlf_kernel(tc, maps, fc1_w, fc1_b, fc2_w, fc2_b, offs, out):
         nc.sync.dma_start(offsets[:], offs)
         stored = [held.tile([P, S], F32, name=f"stored{k}") for k in range(C_BLOCKS)]
         nc.scalar.dma_start(stored[0][:], maps[0:P, :])
+        warmed = held.tile([P, 1], F32, name="warmed")
+        nc.scalar.memzero(warmed[:])
         nc.sync.dma_start(stored[1][:], maps[P : 2 * P, :])
         w1 = held.tile([P, C_BLOCKS, M1], BF16, name="w1")
         nc.sync.dma_start(w1[:], fc1_w.rearrange("(k p) m -> p k m", p=P))
@@ -41,11 +43,6 @@ def tile_rlf_kernel(tc, maps, fc1_w, fc1_b, fc2_w, fc2_b, offs, out):
             nc.gpsimd.dma_start(b1[:], fc1_b.rearrange("(m p) o -> p (m o)", p=P))
         b2 = held.tile([P, 1], F32, name="b2")
         nc.scalar.dma_start(b2[:], fc2_b)
-
-        warm = held.tile([P, 1], F32, name="warm")
-        nc.vector.memset(warm[:], 0.0)
-        warmed = held.tile([P, 1], F32, name="warmed")
-        nc.scalar.activation(warmed[:], warm[:], COPY)
 
         zeros = held.tile([P, WARM_COLUMNS], BF16, name="zeros")
         nc.vector.memset(zeros[:], 0.0)

@@ -4,8 +4,10 @@ P = 128
 C, S, N, M1, M2 = 256, 512, 256, 256, 128
 C_BLOCKS = C // P
 M_BLOCKS = M1 // P
-PIECES = 2
-W = N // PIECES
+WIDTHS = (128, 64, 64)
+STARTS = (0, 128, 192)
+PIECES = len(WIDTHS)
+STORES = 2
 WARM_COLUMNS = 512
 WARM_MATMULS = 6
 SLOPE = 0.2
@@ -18,10 +20,10 @@ IDENTITY = mybir.ActivationFunctionType.Identity
 MULT, MAX = mybir.AluOpType.mult, mybir.AluOpType.max
 
 
-def bias_then_leaky(nc, pool, result, product, bias, name):
-    biased = pool.tile([P, W], F32, name=name)
-    nc.scalar.activation(biased[:], product[:], IDENTITY, bias=bias)
-    nc.vector.scalar_tensor_tensor(result[:], biased[:], SLOPE, biased[:], MULT, MAX)
+def bias_then_leaky(nc, pool, result, product, bias, width, name):
+    biased = pool.tile([P, width], F32, name=name)
+    nc.scalar.activation(biased[:], product, IDENTITY, bias=bias)
+    nc.vector.scalar_tensor_tensor(result, biased[:], SLOPE, biased[:], MULT, MAX)
 
 
 def tile_rlf_kernel(tc, maps, fc1_w, fc1_b, fc2_w, fc2_b, offs, out):
@@ -51,34 +53,46 @@ def tile_rlf_kernel(tc, maps, fc1_w, fc1_b, fc2_w, fc2_b, offs, out):
             nc.tensor.matmul(unread[:], zeros[:, 0:P], zeros[:], start=True, stop=True)
 
         product1 = [
-            [psum.tile([P, W], F32, name=f"product1_{i}_{m}") for m in range(M_BLOCKS)] for i in range(PIECES)
+            [psum.tile([P, WIDTHS[i]], F32, name=f"product1_{i}_{m}") for m in range(M_BLOCKS)] for i in range(PIECES)
         ]
-        for k in range(C_BLOCKS):
-            for i in range(PIECES):
-                z = held.tile([P, W], F32, name=f"z_{k}_{i}")
-                piece_of_list = offsets[:, i * (W // 16) : (i + 1) * (W // 16)]
-                nc.scalar.activation(z[:], stored[k][:].indirect(piece_of_list), COPY)
-                z_bf16 = held.tile([P, W], BF16, name=f"z_bf16_{k}_{i}")
-                nc.vector.tensor_copy(z_bf16[:], z[:])
-                for m in range(M_BLOCKS):
-                    nc.tensor.matmul(
-                        product1[i][m][:],
-                        w1[:, k, m * P : (m + 1) * P],
-                        z_bf16[:],
-                        start=(k == 0),
-                        stop=(k == C_BLOCKS - 1),
-                    )
-
-        h = [[held.tile([P, W], BF16, name=f"h_{i}_{m}") for m in range(M_BLOCKS)] for i in range(PIECES)]
+        z_first = held.tile([P, N], F32, name="z_first")
+        nc.scalar.activation(z_first[:], stored[0][:].indirect(offsets[:]), COPY)
+        z_first_bf16 = held.tile([P, N], BF16, name="z_first_bf16")
+        nc.vector.tensor_copy(z_first_bf16[:], z_first[:])
         for i in range(PIECES):
             for m in range(M_BLOCKS):
-                bias_then_leaky(nc, held, h[i][m], product1[i][m], b1[:, m : m + 1], f"biased1_{i}_{m}")
+                nc.tensor.matmul(
+                    product1[i][m][:],
+                    w1[:, 0, m * P : (m + 1) * P],
+                    z_first_bf16[:, STARTS[i] : STARTS[i] + WIDTHS[i]],
+                    start=True,
+                    stop=False,
+                )
+        for i in range(PIECES):
+            z_last = held.tile([P, WIDTHS[i]], F32, name=f"z_last_{i}")
+            piece_of_list = offsets[:, STARTS[i] // 16 : (STARTS[i] + WIDTHS[i]) // 16]
+            nc.scalar.activation(z_last[:], stored[1][:].indirect(piece_of_list), COPY)
+            z_last_bf16 = held.tile([P, WIDTHS[i]], BF16, name=f"z_last_bf16_{i}")
+            nc.vector.tensor_copy(z_last_bf16[:], z_last[:])
+            for m in range(M_BLOCKS):
+                nc.tensor.matmul(product1[i][m][:], w1[:, 1, m * P : (m + 1) * P], z_last_bf16[:], start=False, stop=True)
 
-        product2 = [psum.tile([P, W], F32, name=f"product2_{i}") for i in range(PIECES)]
+        h = [[held.tile([P, WIDTHS[i]], BF16, name=f"h_{i}_{m}") for m in range(M_BLOCKS)] for i in range(PIECES)]
+        for i in range(PIECES):
+            for m in range(M_BLOCKS):
+                bias_then_leaky(
+                    nc, held, h[i][m][:], product1[i][m][:], b1[:, m : m + 1], WIDTHS[i], f"biased1_{i}_{m}"
+                )
+
+        product2 = [psum.tile([P, WIDTHS[i]], F32, name=f"product2_{i}", tag=f"product1_{i}_0") for i in range(PIECES)]
         for i in range(PIECES):
             for m in range(M_BLOCKS):
                 nc.tensor.matmul(product2[i][:], w2[:, m, :], h[i][m][:], start=(m == 0), stop=(m == M_BLOCKS - 1))
+        result = held.tile([P, N], F32, name="result")
         for i in range(PIECES):
-            result = held.tile([P, W], F32, name=f"result_{i}")
-            bias_then_leaky(nc, held, result, product2[i], b2[:], f"biased2_{i}")
-            nc.sync.dma_start(out[:, i * W : (i + 1) * W], result[:])
+            bias_then_leaky(
+                nc, held, result[:, STARTS[i] : STARTS[i] + WIDTHS[i]], product2[i][:], b2[:], WIDTHS[i], f"biased2_{i}"
+            )
+        for s in range(STORES):
+            samples = slice(s * (N // STORES), (s + 1) * (N // STORES))
+            nc.sync.dma_start(out[:, samples], result[:, samples])

@@ -90,8 +90,10 @@ def tile_rlf_kernel(tc, maps, fc1_w, fc1_b, fc2_w, fc2_b, offs, out):
                 nc.tensor.matmul(product2[i][:], w2[:, m, :], h[i][m][:], start=(m == 0), stop=(m == M_BLOCKS - 1))
         result = held.tile([P, N], F32, name="result")
         for i in range(PIECES):
-            bias_then_leaky(
-                nc, held, result[:, STARTS[i] : STARTS[i] + WIDTHS[i]], product2[i][:], b2[:], WIDTHS[i], f"biased2_{i}"
+            biased2 = held.tile([P, WIDTHS[i]], F32, name=f"biased2_{i}")
+            nc.vector.tensor_scalar_add(biased2[:], product2[i][:], b2[:])
+            nc.vector.scalar_tensor_tensor(
+                result[:, STARTS[i] : STARTS[i] + WIDTHS[i]], biased2[:], SLOPE, biased2[:], MULT, MAX
             )
         for s in range(STORES):
             samples = slice(s * (N // STORES), (s + 1) * (N // STORES))

@@ -4,9 +4,9 @@ P = 128
 C, S, N, M1, M2 = 256, 512, 256, 256, 128
 C_BLOCKS = C // P
 M_BLOCKS = M1 // P
-WIDTHS = (128, 64, 64)
-STARTS = (0, 128, 192)
-PIECES = len(WIDTHS)
+WIDTH = 64
+STARTS = range(0, N, WIDTH)
+PIECES = N // WIDTH
 STORES = 2
 WARM_COLUMNS = 512
 WARM_MATMULS = 6
@@ -48,12 +48,12 @@ def tile_rlf_kernel(tc, maps, fc1_w, fc1_b, fc2_w, fc2_b, offs, out):
 
         zeros = held.tile([P, WARM_COLUMNS], BF16, name="zeros")
         nc.vector.memset(zeros[:], 0.0)
-        unread = psum.tile([P, WARM_COLUMNS], F32, name="unread")
+        unread = psum.tile([P, WARM_COLUMNS], F32, name="unread", tag=f"product1_{PIECES - 1}_{M_BLOCKS - 1}")
         for repeat in range(WARM_MATMULS):
             nc.tensor.matmul(unread[:], zeros[:, 0:P], zeros[:], start=True, stop=True)
 
         product1 = [
-            [psum.tile([P, WIDTHS[i]], F32, name=f"product1_{i}_{m}") for m in range(M_BLOCKS)] for i in range(PIECES)
+            [psum.tile([P, WIDTH], F32, name=f"product1_{i}_{m}") for m in range(M_BLOCKS)] for i in range(PIECES)
         ]
         z_first = held.tile([P, N], F32, name="z_first")
         nc.scalar.activation(z_first[:], stored[0][:].indirect(offsets[:]), COPY)
@@ -64,36 +64,36 @@ def tile_rlf_kernel(tc, maps, fc1_w, fc1_b, fc2_w, fc2_b, offs, out):
                 nc.tensor.matmul(
                     product1[i][m][:],
                     w1[:, 0, m * P : (m + 1) * P],
-                    z_first_bf16[:, STARTS[i] : STARTS[i] + WIDTHS[i]],
+                    z_first_bf16[:, STARTS[i] : STARTS[i] + WIDTH],
                     start=True,
                     stop=False,
                 )
         for i in range(PIECES):
-            z_last = held.tile([P, WIDTHS[i]], F32, name=f"z_last_{i}")
-            piece_of_list = offsets[:, STARTS[i] // 16 : (STARTS[i] + WIDTHS[i]) // 16]
+            z_last = held.tile([P, WIDTH], F32, name=f"z_last_{i}")
+            piece_of_list = offsets[:, STARTS[i] // 16 : (STARTS[i] + WIDTH) // 16]
             nc.scalar.activation(z_last[:], stored[1][:].indirect(piece_of_list), COPY)
-            z_last_bf16 = held.tile([P, WIDTHS[i]], BF16, name=f"z_last_bf16_{i}")
+            z_last_bf16 = held.tile([P, WIDTH], BF16, name=f"z_last_bf16_{i}")
             nc.vector.tensor_copy(z_last_bf16[:], z_last[:])
             for m in range(M_BLOCKS):
                 nc.tensor.matmul(product1[i][m][:], w1[:, 1, m * P : (m + 1) * P], z_last_bf16[:], start=False, stop=True)
 
-        h = [[held.tile([P, WIDTHS[i]], BF16, name=f"h_{i}_{m}") for m in range(M_BLOCKS)] for i in range(PIECES)]
+        h = [[held.tile([P, WIDTH], BF16, name=f"h_{i}_{m}") for m in range(M_BLOCKS)] for i in range(PIECES)]
         for i in range(PIECES):
             for m in range(M_BLOCKS):
                 bias_then_leaky(
-                    nc, held, h[i][m][:], product1[i][m][:], b1[:, m : m + 1], WIDTHS[i], f"biased1_{i}_{m}"
+                    nc, held, h[i][m][:], product1[i][m][:], b1[:, m : m + 1], WIDTH, f"biased1_{i}_{m}"
                 )
 
-        product2 = [psum.tile([P, WIDTHS[i]], F32, name=f"product2_{i}", tag=f"product1_{i}_0") for i in range(PIECES)]
+        product2 = [psum.tile([P, WIDTH], F32, name=f"product2_{i}", tag=f"product1_{i}_0") for i in range(PIECES)]
         for i in range(PIECES):
             for m in range(M_BLOCKS):
                 nc.tensor.matmul(product2[i][:], w2[:, m, :], h[i][m][:], start=(m == 0), stop=(m == M_BLOCKS - 1))
         result = held.tile([P, N], F32, name="result")
         for i in range(PIECES):
-            biased2 = held.tile([P, WIDTHS[i]], F32, name=f"biased2_{i}")
+            biased2 = held.tile([P, WIDTH], F32, name=f"biased2_{i}")
             nc.vector.tensor_scalar_add(biased2[:], product2[i][:], b2[:])
             nc.vector.scalar_tensor_tensor(
-                result[:, STARTS[i] : STARTS[i] + WIDTHS[i]], biased2[:], SLOPE, biased2[:], MULT, MAX
+                result[:, STARTS[i] : STARTS[i] + WIDTH], biased2[:], SLOPE, biased2[:], MULT, MAX
             )
         for s in range(STORES):
             samples = slice(s * (N // STORES), (s + 1) * (N // STORES))

@@ -46,11 +46,11 @@ def tile_rlf_kernel(tc, maps, fc1_w, fc1_b, fc2_w, fc2_b, offs, out):
         b2 = held.tile([P, 1], F32, name="b2")
         nc.scalar.dma_start(b2[:], fc2_b)
 
-        zeros = held.tile([P, WARM_COLUMNS], BF16, name="zeros")
+        zeros = held.tile([P, P], BF16, name="zeros")
         nc.vector.memset(zeros[:], 0.0)
         unread = psum.tile([P, WARM_COLUMNS], F32, name="unread", tag=f"product1_{PIECES - 1}_{M_BLOCKS - 1}")
         for repeat in range(WARM_MATMULS):
-            nc.tensor.matmul(unread[:], zeros[:, 0:P], zeros[:], start=True, stop=True)
+            nc.tensor.matmul(unread[:], zeros[:], zeros[:, 0:1].to_broadcast([P, WARM_COLUMNS]), start=True, stop=True)
 
         product1 = [
             [psum.tile([P, WIDTH], F32, name=f"product1_{i}_{m}") for m in range(M_BLOCKS)] for i in range(PIECES)

import concourse.mybir as mybir

P = 128
C, S, N, M1, M2 = 256, 512, 256, 256, 128
C_BLOCKS = C // P
M_BLOCKS = M1 // P
WIDTH = 64
STARTS = range(0, N, WIDTH)
PIECES = N // WIDTH
STORES = 2
WARM_COLUMNS = 512
WARM_MATMULS = 6
SLOPE = 0.2

FLOPS = 2 * C * M1 * N + 2 * M1 * M2 * N

F32, BF16, U16 = mybir.dt.float32, mybir.dt.bfloat16, mybir.dt.uint16
COPY = mybir.ActivationFunctionType.Copy
IDENTITY = mybir.ActivationFunctionType.Identity
MULT, MAX = mybir.AluOpType.mult, mybir.AluOpType.max


def bias_then_leaky(nc, pool, result, product, bias, width, name):
    biased = pool.tile([P, width], F32, name=name)
    nc.scalar.activation(biased[:], product, IDENTITY, bias=bias)
    nc.vector.scalar_tensor_tensor(result, biased[:], SLOPE, biased[:], MULT, MAX)


def tile_rlf_kernel(tc, maps, fc1_w, fc1_b, fc2_w, fc2_b, offs, out):
    nc = tc.nc
    with tc.tile_pool(name="held", bufs=1) as held, tc.psum_pool(name="psum", bufs=1) as psum:
        offsets = held.tile([P, N // 16], U16, name="offsets")
        nc.sync.dma_start(offsets[:], offs)
        stored = [held.tile([P, S], F32, name=f"stored{k}") for k in range(C_BLOCKS)]
        nc.scalar.dma_start(stored[0][:], maps[0:P, :])
        warmed = held.tile([P, 1], F32, name="warmed")
        nc.scalar.memzero(warmed[:])
        nc.sync.dma_start(stored[1][:], maps[P : 2 * P, :])
        w1 = held.tile([P, C_BLOCKS, M1], BF16, name="w1")
        nc.sync.dma_start(w1[:], fc1_w.rearrange("(k p) m -> p k m", p=P))
        w2 = held.tile([P, M_BLOCKS, M2], BF16, name="w2")
        nc.sync.dma_start(w2[:], fc2_w.rearrange("(k p) q -> p k q", p=P))
        b1 = held.tile([P, M_BLOCKS], F32, name="b1")
        with nc.allow_non_contiguous_dma(reason="a bias has one element to a partition"):
            nc.gpsimd.dma_start(b1[:], fc1_b.rearrange("(m p) o -> p (m o)", p=P))
        b2 = held.tile([P, 1], F32, name="b2")
        nc.scalar.dma_start(b2[:], fc2_b)

        zeros = held.tile([P, P], BF16, name="zeros")
        nc.vector.memset(zeros[:], 0.0)
        unread = psum.tile([P, WARM_COLUMNS], F32, name="unread", tag=f"product1_{PIECES - 1}_{M_BLOCKS - 1}")
        for repeat in range(WARM_MATMULS):
            nc.tensor.matmul(unread[:], zeros[:], zeros[:, 0:1].to_broadcast([P, WARM_COLUMNS]), start=True, stop=True)

        product1 = [
            [psum.tile([P, WIDTH], F32, name=f"product1_{i}_{m}") for m in range(M_BLOCKS)] for i in range(PIECES)
        ]
        z_first = held.tile([P, N], F32, name="z_first")
        nc.scalar.activation(z_first[:], stored[0][:].indirect(offsets[:]), COPY)
        z_first_bf16 = held.tile([P, N], BF16, name="z_first_bf16")
        nc.vector.tensor_copy(z_first_bf16[:], z_first[:])
        for i in range(PIECES):
            for m in range(M_BLOCKS):
                nc.tensor.matmul(
                    product1[i][m][:],
                    w1[:, 0, m * P : (m + 1) * P],
                    z_first_bf16[:, STARTS[i] : STARTS[i] + WIDTH],
                    start=True,
                    stop=False,
                )
        for i in range(PIECES):
            z_last = held.tile([P, WIDTH], F32, name=f"z_last_{i}")
            piece_of_list = offsets[:, STARTS[i] // 16 : (STARTS[i] + WIDTH) // 16]
            nc.scalar.activation(z_last[:], stored[1][:].indirect(piece_of_list), COPY)
            z_last_bf16 = held.tile([P, WIDTH], BF16, name=f"z_last_bf16_{i}")
            nc.vector.tensor_copy(z_last_bf16[:], z_last[:])
            for m in range(M_BLOCKS):
                nc.tensor.matmul(product1[i][m][:], w1[:, 1, m * P : (m + 1) * P], z_last_bf16[:], start=False, stop=True)

        h = [[held.tile([P, WIDTH], BF16, name=f"h_{i}_{m}") for m in range(M_BLOCKS)] for i in range(PIECES)]
        for i in range(PIECES):
            for m in range(M_BLOCKS):
                bias_then_leaky(
                    nc, held, h[i][m][:], product1[i][m][:], b1[:, m : m + 1], WIDTH, f"biased1_{i}_{m}"
                )

        product2 = [psum.tile([P, WIDTH], F32, name=f"product2_{i}", tag=f"product1_{i}_0") for i in range(PIECES)]
        for i in range(PIECES):
            for m in range(M_BLOCKS):
                nc.tensor.matmul(product2[i][:], w2[:, m, :], h[i][m][:], start=(m == 0), stop=(m == M_BLOCKS - 1))
        result = held.tile([P, N], F32, name="result")
        for i in range(PIECES):
            biased2 = held.tile([P, WIDTH], F32, name=f"biased2_{i}")
            nc.vector.tensor_scalar_add(biased2[:], product2[i][:], b2[:])
            nc.vector.scalar_tensor_tensor(
                result[:, STARTS[i] : STARTS[i] + WIDTH], biased2[:], SLOPE, biased2[:], MULT, MAX
            )
        for s in range(STORES):
            samples = slice(s * (N // STORES), (s + 1) * (N // STORES))
            nc.sync.dma_start(out[:, samples], result[:, samples])
